import numpy as np
import ml_dtypes


def mxq(x, axis, fmt="e4m3"):
    dtype, down = {"e4m3": (ml_dtypes.float8_e4m3fn, 7), "e5m2": (ml_dtypes.float8_e5m2, 14)}[fmt]
    v = np.moveaxis(np.asarray(x, np.float32).astype(ml_dtypes.bfloat16).astype(np.float64), axis, -1)
    blocks = v.reshape(v.shape[:-1] + (-1, 32))
    amax = np.abs(blocks).max(-1, keepdims=True)
    byte = np.maximum(np.where(amax > 0, np.frexp(amax)[1] - 1 + 127, 0) - down, 1)
    scale = np.exp2(byte - 127.0)
    codes = (blocks / scale).astype(np.float32).astype(dtype).astype(np.float64)
    return np.moveaxis((codes * scale).reshape(v.shape), -1, axis)


WIDE = False


def mx_kscale(k):
    if not WIDE:
        return np.ones(k)
    levels = np.array([10, -10, 5, -5, 0])
    a = np.random.permutation(np.resize(levels, k // 512 * 4)).reshape(k // 512, 4)
    idx = np.arange(k)
    return np.exp2(a[idx // 512, idx % 128 // 32])


BF16 = ml_dtypes.bfloat16


def bf(x):
    return np.asarray(x, np.float32).astype(BF16)


def f64(x):
    return np.asarray(x).astype(np.float64)


B, H, D, DV, N = 1, 1, 512, 1024, 4096
DIM = H * DV


def setup_inputs():
    s, t = mx_kscale(N), mx_kscale(D)
    c = np.exp2(np.round(np.log2(s.mean())))
    q = (np.random.standard_normal((B, H, D, N)) - 1.0) * 3.0 / np.sqrt(D) / t[:, None]
    k = (np.random.standard_normal((B, H, D, N)) - 1.0) * 3.0 / np.sqrt(N) * t[:, None] * s
    v = np.random.standard_normal((B, H, DV, N)) * 0.125 * np.sqrt(N) * c / s
    return {"q": bf(q), "k": bf(k), "v": bf(v)}


def reference(q, k, v):
    qr = np.maximum(f64(q), 0.0)
    kr = np.maximum(f64(k), 0.0)
    vk = mxq(f64(v), 3, "e4m3") @ mxq(kr, 3, "e4m3").transpose(0, 1, 3, 2)
    ksum = kr.sum(-1)
    num = mxq(vk, 3, "e4m3") @ mxq(qr, 2, "e4m3")
    den = (ksum[..., None] * qr).sum(-2, keepdims=True)
    out = num / den
    return out.transpose(0, 2, 1, 3).reshape(B, -1, DIM)

@@ -1,0 +1,253 @@
+from contextlib import ExitStack
+
+import concourse.mybir as mybir
+from concourse.masks import make_identity
+
+F32 = mybir.dt.float32
+BF16 = mybir.dt.bfloat16
+U32 = mybir.dt.uint32
+U8 = mybir.dt.uint8
+FP8X4 = mybir.dt.float8_e4m3fn_x4
+ACT = mybir.ActivationFunctionType
+ALU = mybir.AluOpType
+AXIS = mybir.AxisListType
+
+P = 128
+PACK = 4
+K_PASS = P * PACK
+E = 512
+DV = 1024
+N = 4096
+E_TILES = E // P
+D_TILES = DV // P
+TOKEN_PASSES = N // K_PASS
+N_TILE = 512
+K_PIECES = 4
+PIECE = N // K_PIECES
+Q_RANGES = 4
+TOKEN_TILES = N // P
+STORE = 2048
+V_BUFS = 4
+AHEAD = 4
+EARLY = 2
+
+FLOPS = 2 * DV * E * N * 2 + 2 * E * N
+
+
+def tile_relu_linear_att_pa_t_kernel(tc, q, k, v, out):
+    nc = tc.nc
+    q_rows = q.rearrange("b h e n -> (b h e) n")
+    k_rows = k.rearrange("b h e n -> (b h e) n")
+    v_rows = v.rearrange("b h d n -> (b h d) n")
+    out_rows = out.rearrange("b (d x) c -> (b d) (x c)", x=N // DV)
+
+    with ExitStack() as ctx:
+        keep = ctx.enter_context(tc.tile_pool(name="keep", bufs=1))
+        v_in = ctx.enter_context(tc.tile_pool(name="v_in", bufs=V_BUFS))
+        grouped_pool = ctx.enter_context(tc.tile_pool(name="grouped", bufs=3))
+        v_mx = ctx.enter_context(tc.tile_pool(name="v_mx", bufs=2))
+        vk_pool = ctx.enter_context(tc.tile_pool(name="vk", bufs=2))
+        rep_pool = ctx.enter_context(tc.tile_pool(name="rep", bufs=2))
+        psum = ctx.enter_context(tc.psum_pool(name="psum", bufs=1))
+
+        ident_f32 = keep.tile([P, P], F32)
+        make_identity(nc, ident_f32[:])
+        ident_bf16 = keep.tile([P, P], BF16)
+        make_identity(nc, ident_bf16[:])
+
+        k_codes = keep.tile([P, TOKEN_PASSES * E], U32, align_bytes=64)
+        k_scales = keep.tile([P, TOKEN_PASSES * E], U8, align_bytes=64)
+        q_codes = keep.tile([P, N], U32, align_bytes=64)
+        q_scales = keep.tile([P, N], U8, align_bytes=64)
+        vk_codes = keep.tile([P, DV], U32, align_bytes=64)
+        vk_scales = keep.tile([P, DV], U8, align_bytes=64)
+        q_sb = keep.tile([P, E_TILES, N], BF16)
+        rden_all = keep.tile([P, N], F32)
+        ksum_parts = keep.tile([P, E_TILES, K_PIECES], F32)
+        ksum = keep.tile([P, E_TILES], F32)
+        pieces = keep.tile([P, E_TILES, 4], BF16)
+        rest1 = keep.tile([P, E_TILES], F32)
+        rest2 = keep.tile([P, E_TILES], F32)
+        den = keep.tile([P, TOKEN_TILES], F32)
+        rden = keep.tile([P, TOKEN_TILES], F32)
+
+        def transpose_words(bank, words, first_word):
+            for g in range(2):
+                for u in range(2):
+                    w0 = first_word + (2 * g + u) * P
+                    nc.tensor.transpose(bank[:, g, u, :], words[:, w0 : w0 + P], ident_f32[:])
+
+        v_tiles = {}
+
+        def load_v(m):
+            v_sb = v_in.tile([P, N], BF16, name="v_sb")
+            nc.sync.dma_start(out=v_sb[:], in_=v_rows[m * P : (m + 1) * P, :])
+            v_tiles[m] = v_sb
+
+        def key_value_state(m):
+            words = v_tiles[m][:].bitcast(F32)
+            grouped = grouped_pool.tile([P, PACK * TOKEN_PASSES * P], BF16, tag="grouped", align_bytes=64)
+            grouped_words = grouped[:].bitcast(F32).rearrange("p (g d u) -> p g d u", g=TOKEN_PASSES, u=2)
+            for b in range(TOKEN_PASSES // 2):
+                bank = psum.tile([P, 2, 2, P], F32, tag="tp", bufs=3)
+                transpose_words(bank, words, 2 * b * (K_PASS // 2))
+                nc.scalar.copy(
+                    out=grouped_words[:, 2 * b : 2 * b + 2, :, :], in_=bank[:].rearrange("p g u d -> p g d u")
+                )
+            codes = v_mx.tile([P, TOKEN_PASSES * P], U32, tag="v_codes", align_bytes=64)
+            scales = v_mx.tile([P, TOKEN_PASSES * P], U8, tag="v_scales", align_bytes=64)
+            nc.vector.quantize_mx(out=codes[:].bitcast(FP8X4), scales=scales[:], in_=grouped[:])
+            vk_ps = psum.tile([P, E], F32, tag="vk_ps", bufs=1)
+            for g in range(TOKEN_PASSES):
+                nc.tensor.matmul_mx(
+                    out=vk_ps[:],
+                    lhsT=codes[:, g * P : (g + 1) * P].bitcast(FP8X4),
+                    lhsT_scale=scales[:, g * P : (g + 1) * P],
+                    rhs=k_codes[:, g * E : (g + 1) * E].bitcast(FP8X4),
+                    rhs_scale=k_scales[:, g * E : (g + 1) * E],
+                    start=(g == 0),
+                    stop=(g == TOKEN_PASSES - 1),
+                )
+            vk_bf = vk_pool.tile([P, E], BF16, tag="vk_bf")
+            nc.scalar.copy(out=vk_bf[:], in_=vk_ps[:])
+            vk_t = psum.tile([P, E_TILES, P], BF16, tag="vk_t", bufs=1)
+            for t in range(E_TILES):
+                nc.tensor.transpose(vk_t[:, t, :], vk_bf[:, t * P : (t + 1) * P], ident_bf16[:])
+            vk_grouped = vk_pool.tile([P, P, PACK], BF16, tag="vk_grouped", align_bytes=64)
+            nc.vector.tensor_copy(out=vk_grouped[:], in_=vk_t[:].rearrange("p t d -> p d t"))
+            cols = slice(m * P, (m + 1) * P)
+            nc.vector.quantize_mx(
+                out=vk_codes[:, cols].bitcast(FP8X4),
+                scales=vk_scales[:, cols],
+                in_=vk_grouped[:].rearrange("p d t -> p (d t)"),
+            )
+
+        with tc.tile_pool(name="k_in", bufs=1) as k_in:
+            k_raw = []
+            for c in range(K_PIECES):
+                piece = k_in.tile([P, E_TILES, PIECE], BF16, tag="k_raw", bufs=K_PIECES, name="piece")
+                nc.sync.dma_start(
+                    out=piece[:],
+                    in_=k_rows.rearrange("(t p) n -> p t n", p=P)[:, :, c * PIECE : (c + 1) * PIECE],
+                )
+                k_raw.append(piece)
+            for m in range(EARLY):
+                load_v(m)
+            for t in range(E_TILES):
+                nc.sync.dma_start(out=q_sb[:, t, :], in_=q_rows[t * P : (t + 1) * P, :])
+            for m in range(EARLY, V_BUFS):
+                load_v(m)
+
+            for c in range(K_PIECES):
+                kr = k_in.tile([P, E_TILES, PIECE], BF16, tag="kr", bufs=2)
+                grouped = grouped_pool.tile([P, PACK * 2 * E], BF16, tag="grouped", align_bytes=64)
+                grouped_words = grouped[:].bitcast(F32).rearrange("p (g e u) -> p g e u", g=2, u=2)
+                for t in range(E_TILES):
+                    nc.vector.tensor_scalar(
+                        out=kr[:, t, :],
+                        in0=k_raw[c][:, t, :],
+                        scalar1=0.0,
+                        scalar2=None,
+                        op0=ALU.max,
+                        op1=ALU.add,
+                        accum_out=ksum_parts[:, t, c : c + 1],
+                    )
+                    bank = psum.tile([P, 2, 2, P], F32, tag="tp", bufs=3)
+                    transpose_words(bank, kr[:, t, :].bitcast(F32), 0)
+                    nc.scalar.copy(
+                        out=grouped_words[:, :, t * P : (t + 1) * P, :],
+                        in_=bank[:].rearrange("p g u e -> p g e u"),
+                    )
+                cols = slice(c * 2 * E, (c + 1) * 2 * E)
+                nc.vector.quantize_mx(out=k_codes[:, cols].bitcast(FP8X4), scales=k_scales[:, cols], in_=grouped[:])
+
+        staging = ctx.enter_context(tc.tile_pool(name="staging", bufs=4))
+
+        for m in range(EARLY):
+            key_value_state(m)
+            load_v(m + V_BUFS)
+
+        for t in range(E_TILES):
+            nc.vector.tensor_scalar_max(out=q_sb[:, t, :], in0=q_sb[:, t, :], scalar1=0.0)
+
+        for r in range(Q_RANGES):
+            width = N // Q_RANGES
+            grouped = grouped_pool.tile([P, PACK * width], BF16, tag="grouped", align_bytes=64)
+            dst = grouped[:].rearrange("p (c i t) -> p c t i", i=4, t=PACK)
+            src = q_sb[:, :, r * width : (r + 1) * width].rearrange("p t (c i) -> p c t i", i=4)
+            if r % 2 == 0:
+                nc.vector.tensor_copy(out=dst, in_=src)
+            else:
+                nc.scalar.copy(out=dst, in_=src)
+            cols = slice(r * width, (r + 1) * width)
+            nc.vector.quantize_mx(out=q_codes[:, cols].bitcast(FP8X4), scales=q_scales[:, cols], in_=grouped[:])
+
+        nc.vector.tensor_reduce(out=ksum[:], in_=ksum_parts[:], axis=AXIS.X, op=ALU.add)
+        nc.vector.memset(pieces[:], 0.0)
+        nc.vector.tensor_copy(out=pieces[:, :, 0], in_=ksum[:])
+        nc.vector.tensor_sub(out=rest1[:], in0=ksum[:], in1=pieces[:, :, 0])
+        nc.vector.tensor_copy(out=pieces[:, :, 1], in_=rest1[:])
+        nc.vector.tensor_sub(out=rest2[:], in0=rest1[:], in1=pieces[:, :, 1])
+        nc.vector.tensor_copy(out=pieces[:, :, 2], in_=rest2[:])
+        den_ps = psum.tile([P, TOKEN_TILES, 4], F32, tag="tp", bufs=3)
+        for j in range(TOKEN_TILES):
+            for t in range(E_TILES):
+                nc.tensor.matmul(
+                    out=den_ps[:, j, :],
+                    lhsT=q_sb[:, t, j * P : (j + 1) * P],
+                    rhs=pieces[:, t, :],
+                    start=(t == 0),
+                    stop=(t == E_TILES - 1),
+                )
+        nc.vector.tensor_reduce(out=den[:], in_=den_ps[:], axis=AXIS.X, op=ALU.add)
+        nc.vector.reciprocal(out=rden[:], in_=den[:])
+        for a in range(TOKEN_TILES // 8):
+            rep = rep_pool.tile([P, 8, P], F32)
+            nc.gpsimd.tensor_scalar(
+                out=rep[:],
+                in0=rden[:, 8 * a : 8 * a + 8].unsqueeze(2).to_broadcast([P, 8, P]),
+                scalar1=1.0,
+                scalar2=0.0,
+                op0=ALU.mult,
+                op1=ALU.add,
+            )
+            for h in range(2):
+                bank = psum.tile([P, 4, P], F32, tag="tp", bufs=3)
+                for i in range(4):
+                    nc.tensor.transpose(bank[:, i, :], rep[:, 4 * h + i, :], ident_f32[:])
+                first = (8 * a + 4 * h) * P
+                nc.scalar.copy(out=rden_all[:, first : first + 4 * P], in_=bank[:].rearrange("p i c -> p (i c)"))
+
+        for m in range(EARLY, AHEAD):
+            key_value_state(m)
+            load_v(m + V_BUFS)
+
+        def attend(m):
+            d_cols = slice(m * P, (m + 1) * P)
+            for s in range(N // STORE):
+                result = staging.tile([P, STORE], F32, tag="result")
+                for i in range(STORE // N_TILE):
+                    j = s * (STORE // N_TILE) + i
+                    n_cols = slice(j * N_TILE, (j + 1) * N_TILE)
+                    num = psum.tile([P, N_TILE], F32, tag="num", bufs=3)
+                    nc.tensor.matmul_mx(
+                        out=num[:],
+                        lhsT=vk_codes[:, d_cols].bitcast(FP8X4),
+                        lhsT_scale=vk_scales[:, d_cols],
+                        rhs=q_codes[:, n_cols].bitcast(FP8X4),
+                        rhs_scale=q_scales[:, n_cols],
+                        start=True,
+                        stop=True,
+                    )
+                    part = result[:, i * N_TILE : (i + 1) * N_TILE]
+                    if j % 3 == 1:
+                        nc.scalar.copy(out=part, in_=num[:])
+                        nc.gpsimd.tensor_mul(out=part, in0=part, in1=rden_all[:, n_cols])
+                    else:
+                        nc.vector.tensor_mul(out=part, in0=num[:], in1=rden_all[:, n_cols])
+                nc.sync.dma_start(out=out_rows[d_cols, s * STORE : (s + 1) * STORE], in_=result[:])
+
+        for m in range(D_TILES):
+            attend(m)
+            if m + AHEAD < D_TILES:
+                key_value_state(m + AHEAD)

@@ -22,14 +22,16 @@ E_TILES = E // P
 D_TILES = DV // P
 TOKEN_PASSES = N // K_PASS
 N_TILE = 512
+N_TILES = N // N_TILE
 K_PIECES = 4
 PIECE = N // K_PIECES
 Q_RANGES = 4
-TOKEN_TILES = N // P
+RANGE = N // Q_RANGES
+RANGE_TILES = RANGE // P
 STORE = 2048
-V_BUFS = 4
-AHEAD = 4
-EARLY = 2
+V_BUFS = 6
+BANKS = 6
+OUT_PER_ROUND = 2
 
 FLOPS = 2 * DV * E * N * 2 + 2 * E * N
 
@@ -42,6 +44,7 @@ def tile_relu_linear_att_pa_t_kernel(tc, q, k, v, out):
     out_rows = out.rearrange("b (d x) c -> (b d) (x c)", x=N // DV)
 
     with ExitStack() as ctx:
+        ctx.enter_context(tc.manual_schedule())
         keep = ctx.enter_context(tc.tile_pool(name="keep", bufs=1))
         v_in = ctx.enter_context(tc.tile_pool(name="v_in", bufs=V_BUFS))
         grouped_pool = ctx.enter_context(tc.tile_pool(name="grouped", bufs=3))
@@ -61,15 +64,18 @@ def tile_relu_linear_att_pa_t_kernel(tc, q, k, v, out):
         q_scales = keep.tile([P, N], U8, align_bytes=64)
         vk_codes = keep.tile([P, DV], U32, align_bytes=64)
         vk_scales = keep.tile([P, DV], U8, align_bytes=64)
-        q_sb = keep.tile([P, E_TILES, N], BF16)
+        q_ranges = [keep.tile([P, E_TILES, RANGE], BF16, name="q_sb%d" % r) for r in range(Q_RANGES)]
         rden_all = keep.tile([P, N], F32)
         ksum_parts = keep.tile([P, E_TILES, K_PIECES], F32)
         ksum = keep.tile([P, E_TILES], F32)
         pieces = keep.tile([P, E_TILES, 4], BF16)
         rest1 = keep.tile([P, E_TILES], F32)
         rest2 = keep.tile([P, E_TILES], F32)
-        den = keep.tile([P, TOKEN_TILES], F32)
-        rden = keep.tile([P, TOKEN_TILES], F32)
+        den = keep.tile([P, Q_RANGES, RANGE_TILES], F32)
+        rden = keep.tile([P, Q_RANGES, RANGE_TILES], F32)
+
+        def new_bank(shape):
+            return psum.tile(shape, F32, tag="bank", bufs=BANKS, name="bank")
 
         def transpose_words(bank, words, first_word):
             for g in range(2):
@@ -78,43 +84,63 @@ def tile_relu_linear_att_pa_t_kernel(tc, q, k, v, out):
                     nc.tensor.transpose(bank[:, g, u, :], words[:, w0 : w0 + P], ident_f32[:])
 
         v_tiles = {}
+        v_grouped = {}
+        v_quantised = {}
+        vk_sums = {}
+        vk_rounded = {}
+        vk_turned = {}
 
         def load_v(m):
             v_sb = v_in.tile([P, N], BF16, name="v_sb")
             nc.sync.dma_start(out=v_sb[:], in_=v_rows[m * P : (m + 1) * P, :])
             v_tiles[m] = v_sb
 
-        def key_value_state(m):
+        def transpose_v(m):
             words = v_tiles[m][:].bitcast(F32)
             grouped = grouped_pool.tile([P, PACK * TOKEN_PASSES * P], BF16, tag="grouped", align_bytes=64)
             grouped_words = grouped[:].bitcast(F32).rearrange("p (g d u) -> p g d u", g=TOKEN_PASSES, u=2)
             for b in range(TOKEN_PASSES // 2):
-                bank = psum.tile([P, 2, 2, P], F32, tag="tp", bufs=3)
+                bank = new_bank([P, 2, 2, P])
                 transpose_words(bank, words, 2 * b * (K_PASS // 2))
                 nc.scalar.copy(
                     out=grouped_words[:, 2 * b : 2 * b + 2, :, :], in_=bank[:].rearrange("p g u d -> p g d u")
                 )
+            v_grouped[m] = grouped
+
+        def quantise_v(m):
             codes = v_mx.tile([P, TOKEN_PASSES * P], U32, tag="v_codes", align_bytes=64)
             scales = v_mx.tile([P, TOKEN_PASSES * P], U8, tag="v_scales", align_bytes=64)
-            nc.vector.quantize_mx(out=codes[:].bitcast(FP8X4), scales=scales[:], in_=grouped[:])
-            vk_ps = psum.tile([P, E], F32, tag="vk_ps", bufs=1)
-            for g in range(TOKEN_PASSES):
-                nc.tensor.matmul_mx(
-                    out=vk_ps[:],
-                    lhsT=codes[:, g * P : (g + 1) * P].bitcast(FP8X4),
-                    lhsT_scale=scales[:, g * P : (g + 1) * P],
-                    rhs=k_codes[:, g * E : (g + 1) * E].bitcast(FP8X4),
-                    rhs_scale=k_scales[:, g * E : (g + 1) * E],
-                    start=(g == 0),
-                    stop=(g == TOKEN_PASSES - 1),
-                )
+            nc.vector.quantize_mx(out=codes[:].bitcast(FP8X4), scales=scales[:], in_=v_grouped[m][:])
+            v_quantised[m] = (codes, scales)
+
+        def state_pass(m, g):
+            if g == 0:
+                vk_sums[m] = psum.tile([P, E], F32, tag="vk_ps", bufs=1, name="vk_ps")
+            codes, scales = v_quantised[m]
+            nc.tensor.matmul_mx(
+                out=vk_sums[m][:],
+                lhsT=codes[:, g * P : (g + 1) * P].bitcast(FP8X4),
+                lhsT_scale=scales[:, g * P : (g + 1) * P],
+                rhs=k_codes[:, g * E : (g + 1) * E].bitcast(FP8X4),
+                rhs_scale=k_scales[:, g * E : (g + 1) * E],
+                start=(g == 0),
+                stop=(g == TOKEN_PASSES - 1),
+            )
+
+        def round_state(m):
             vk_bf = vk_pool.tile([P, E], BF16, tag="vk_bf")
-            nc.scalar.copy(out=vk_bf[:], in_=vk_ps[:])
+            nc.scalar.copy(out=vk_bf[:], in_=vk_sums[m][:])
+            vk_rounded[m] = vk_bf
+
+        def transpose_state(m):
             vk_t = psum.tile([P, E_TILES, P], BF16, tag="vk_t", bufs=1)
             for t in range(E_TILES):
-                nc.tensor.transpose(vk_t[:, t, :], vk_bf[:, t * P : (t + 1) * P], ident_bf16[:])
+                nc.tensor.transpose(vk_t[:, t, :], vk_rounded[m][:, t * P : (t + 1) * P], ident_bf16[:])
+            vk_turned[m] = vk_t
+
+        def quantise_state(m):
             vk_grouped = vk_pool.tile([P, P, PACK], BF16, tag="vk_grouped", align_bytes=64)
-            nc.vector.tensor_copy(out=vk_grouped[:], in_=vk_t[:].rearrange("p t d -> p d t"))
+            nc.vector.tensor_copy(out=vk_grouped[:], in_=vk_turned[m][:].rearrange("p t d -> p d t"))
             cols = slice(m * P, (m + 1) * P)
             nc.vector.quantize_mx(
                 out=vk_codes[:, cols].bitcast(FP8X4),
@@ -122,132 +148,196 @@ def tile_relu_linear_att_pa_t_kernel(tc, q, k, v, out):
                 in_=vk_grouped[:].rearrange("p d t -> p (d t)"),
             )
 
-        with tc.tile_pool(name="k_in", bufs=1) as k_in:
-            k_raw = []
-            for c in range(K_PIECES):
-                piece = k_in.tile([P, E_TILES, PIECE], BF16, tag="k_raw", bufs=K_PIECES, name="piece")
-                nc.sync.dma_start(
-                    out=piece[:],
-                    in_=k_rows.rearrange("(t p) n -> p t n", p=P)[:, :, c * PIECE : (c + 1) * PIECE],
-                )
-                k_raw.append(piece)
-            for m in range(EARLY):
-                load_v(m)
-            for t in range(E_TILES):
-                nc.sync.dma_start(out=q_sb[:, t, :], in_=q_rows[t * P : (t + 1) * P, :])
-            for m in range(EARLY, V_BUFS):
-                load_v(m)
+        q_grouped = {}
+        den_sums = {}
+        repeated = {}
 
-            for c in range(K_PIECES):
-                kr = k_in.tile([P, E_TILES, PIECE], BF16, tag="kr", bufs=2)
-                grouped = grouped_pool.tile([P, PACK * 2 * E], BF16, tag="grouped", align_bytes=64)
-                grouped_words = grouped[:].bitcast(F32).rearrange("p (g e u) -> p g e u", g=2, u=2)
+        def relu_q(r):
+            nc.vector.tensor_scalar_max(out=q_ranges[r][:], in0=q_ranges[r][:], scalar1=0.0)
+
+        def regroup_q(r):
+            grouped = grouped_pool.tile([P, PACK * RANGE], BF16, tag="grouped", align_bytes=64)
+            half = RANGE // 2
+            for s in range(2):
+                dst = grouped[:, s * PACK * half : (s + 1) * PACK * half].rearrange("p (c i t) -> p c t i", i=4, t=PACK)
+                src = q_ranges[r][:, :, s * half : (s + 1) * half].rearrange("p t (c i) -> p c t i", i=4)
+                if s == 0:
+                    nc.vector.tensor_copy(out=dst, in_=src)
+                else:
+                    nc.scalar.copy(out=dst, in_=src)
+            q_grouped[r] = grouped
+
+        def quantise_q(r):
+            cols = slice(r * RANGE, (r + 1) * RANGE)
+            nc.vector.quantize_mx(out=q_codes[:, cols].bitcast(FP8X4), scales=q_scales[:, cols], in_=q_grouped[r][:])
+
+        def den_matmuls(r):
+            den_ps = new_bank([P, RANGE_TILES, 4])
+            for j in range(RANGE_TILES):
                 for t in range(E_TILES):
-                    nc.vector.tensor_scalar(
-                        out=kr[:, t, :],
-                        in0=k_raw[c][:, t, :],
-                        scalar1=0.0,
-                        scalar2=None,
-                        op0=ALU.max,
-                        op1=ALU.add,
-                        accum_out=ksum_parts[:, t, c : c + 1],
+                    nc.tensor.matmul(
+                        out=den_ps[:, j, :],
+                        lhsT=q_ranges[r][:, t, j * P : (j + 1) * P],
+                        rhs=pieces[:, t, :],
+                        start=(t == 0),
+                        stop=(t == E_TILES - 1),
                     )
-                    bank = psum.tile([P, 2, 2, P], F32, tag="tp", bufs=3)
-                    transpose_words(bank, kr[:, t, :].bitcast(F32), 0)
-                    nc.scalar.copy(
-                        out=grouped_words[:, :, t * P : (t + 1) * P, :],
-                        in_=bank[:].rearrange("p g u e -> p g e u"),
-                    )
-                cols = slice(c * 2 * E, (c + 1) * 2 * E)
-                nc.vector.quantize_mx(out=k_codes[:, cols].bitcast(FP8X4), scales=k_scales[:, cols], in_=grouped[:])
+            den_sums[r] = den_ps
 
-        staging = ctx.enter_context(tc.tile_pool(name="staging", bufs=4))
-
-        for m in range(EARLY):
-            key_value_state(m)
-            load_v(m + V_BUFS)
-
-        for t in range(E_TILES):
-            nc.vector.tensor_scalar_max(out=q_sb[:, t, :], in0=q_sb[:, t, :], scalar1=0.0)
-
-        for r in range(Q_RANGES):
-            width = N // Q_RANGES
-            grouped = grouped_pool.tile([P, PACK * width], BF16, tag="grouped", align_bytes=64)
-            dst = grouped[:].rearrange("p (c i t) -> p c t i", i=4, t=PACK)
-            src = q_sb[:, :, r * width : (r + 1) * width].rearrange("p t (c i) -> p c t i", i=4)
-            if r % 2 == 0:
-                nc.vector.tensor_copy(out=dst, in_=src)
-            else:
-                nc.scalar.copy(out=dst, in_=src)
-            cols = slice(r * width, (r + 1) * width)
-            nc.vector.quantize_mx(out=q_codes[:, cols].bitcast(FP8X4), scales=q_scales[:, cols], in_=grouped[:])
-
-        nc.vector.tensor_reduce(out=ksum[:], in_=ksum_parts[:], axis=AXIS.X, op=ALU.add)
-        nc.vector.memset(pieces[:], 0.0)
-        nc.vector.tensor_copy(out=pieces[:, :, 0], in_=ksum[:])
-        nc.vector.tensor_sub(out=rest1[:], in0=ksum[:], in1=pieces[:, :, 0])
-        nc.vector.tensor_copy(out=pieces[:, :, 1], in_=rest1[:])
-        nc.vector.tensor_sub(out=rest2[:], in0=rest1[:], in1=pieces[:, :, 1])
-        nc.vector.tensor_copy(out=pieces[:, :, 2], in_=rest2[:])
-        den_ps = psum.tile([P, TOKEN_TILES, 4], F32, tag="tp", bufs=3)
-        for j in range(TOKEN_TILES):
-            for t in range(E_TILES):
-                nc.tensor.matmul(
-                    out=den_ps[:, j, :],
-                    lhsT=q_sb[:, t, j * P : (j + 1) * P],
-                    rhs=pieces[:, t, :],
-                    start=(t == 0),
-                    stop=(t == E_TILES - 1),
-                )
-        nc.vector.tensor_reduce(out=den[:], in_=den_ps[:], axis=AXIS.X, op=ALU.add)
-        nc.vector.reciprocal(out=rden[:], in_=den[:])
-        for a in range(TOKEN_TILES // 8):
-            rep = rep_pool.tile([P, 8, P], F32)
+        def reciprocal_den(r):
+            nc.vector.tensor_reduce(out=den[:, r, :], in_=den_sums[r][:], axis=AXIS.X, op=ALU.add)
+            nc.vector.reciprocal(out=rden[:, r, :], in_=den[:, r, :])
+            rep = rep_pool.tile([P, RANGE_TILES, P], F32)
             nc.gpsimd.tensor_scalar(
                 out=rep[:],
-                in0=rden[:, 8 * a : 8 * a + 8].unsqueeze(2).to_broadcast([P, 8, P]),
+                in0=rden[:, r, :].unsqueeze(2).to_broadcast([P, RANGE_TILES, P]),
                 scalar1=1.0,
                 scalar2=0.0,
                 op0=ALU.mult,
                 op1=ALU.add,
             )
-            for h in range(2):
-                bank = psum.tile([P, 4, P], F32, tag="tp", bufs=3)
-                for i in range(4):
-                    nc.tensor.transpose(bank[:, i, :], rep[:, 4 * h + i, :], ident_f32[:])
-                first = (8 * a + 4 * h) * P
-                nc.scalar.copy(out=rden_all[:, first : first + 4 * P], in_=bank[:].rearrange("p i c -> p (i c)"))
+            repeated[r] = rep
 
-        for m in range(EARLY, AHEAD):
-            key_value_state(m)
-            load_v(m + V_BUFS)
+        def spread_den(r):
+            for h in range(RANGE // N_TILE):
+                bank = new_bank([P, N_TILE // P, P])
+                for i in range(N_TILE // P):
+                    nc.tensor.transpose(bank[:, i, :], repeated[r][:, h * (N_TILE // P) + i, :], ident_f32[:])
+                first = r * RANGE + h * N_TILE
+                nc.scalar.copy(out=rden_all[:, first : first + N_TILE], in_=bank[:].rearrange("p i c -> p (i c)"))
 
-        def attend(m):
-            d_cols = slice(m * P, (m + 1) * P)
-            for s in range(N // STORE):
-                result = staging.tile([P, STORE], F32, tag="result")
-                for i in range(STORE // N_TILE):
-                    j = s * (STORE // N_TILE) + i
-                    n_cols = slice(j * N_TILE, (j + 1) * N_TILE)
-                    num = psum.tile([P, N_TILE], F32, tag="num", bufs=3)
-                    nc.tensor.matmul_mx(
-                        out=num[:],
-                        lhsT=vk_codes[:, d_cols].bitcast(FP8X4),
-                        lhsT_scale=vk_scales[:, d_cols],
-                        rhs=q_codes[:, n_cols].bitcast(FP8X4),
-                        rhs_scale=q_scales[:, n_cols],
-                        start=True,
-                        stop=True,
+        with tc.tile_pool(name="k_in", bufs=K_PIECES) as k_in:
+            k_pieces = []
+            for c in range(K_PIECES):
+                piece = k_in.tile([P, E_TILES, PIECE], BF16, name="piece")
+                nc.sync.dma_start(
+                    out=piece[:],
+                    in_=k_rows.rearrange("(t p) n -> p t n", p=P)[:, :, c * PIECE : (c + 1) * PIECE],
+                )
+                k_pieces.append(piece)
+
+            def load_q(r):
+                nc.sync.dma_start(
+                    out=q_ranges[r][:],
+                    in_=q_rows.rearrange("(t p) n -> p t n", p=P)[:, :, r * RANGE : (r + 1) * RANGE],
+                )
+
+            load_v(0)
+            load_v(1)
+            load_q(0)
+            load_q(1)
+            load_v(2)
+            load_q(2)
+            load_v(3)
+            load_q(3)
+            load_v(4)
+            load_v(5)
+
+            k_grouped = {}
+            for c in range(K_PIECES + 1):
+                if c < K_PIECES:
+                    kr = k_pieces[c]
+                    grouped = grouped_pool.tile([P, PACK * 2 * E], BF16, tag="grouped", align_bytes=64)
+                    grouped_words = grouped[:].bitcast(F32).rearrange("p (g e u) -> p g e u", g=2, u=2)
+                    for t in range(E_TILES):
+                        nc.vector.tensor_scalar(
+                            out=kr[:, t, :],
+                            in0=kr[:, t, :],
+                            scalar1=0.0,
+                            scalar2=None,
+                            op0=ALU.max,
+                            op1=ALU.add,
+                            accum_out=ksum_parts[:, t, c : c + 1],
+                        )
+                        bank = new_bank([P, 2, 2, P])
+                        transpose_words(bank, kr[:, t, :].bitcast(F32), 0)
+                        nc.scalar.copy(
+                            out=grouped_words[:, :, t * P : (t + 1) * P, :],
+                            in_=bank[:].rearrange("p g u e -> p g e u"),
+                        )
+                    k_grouped[c] = grouped
+                if c == K_PIECES:
+                    nc.vector.tensor_reduce(out=ksum[:], in_=ksum_parts[:], axis=AXIS.X, op=ALU.add)
+                    nc.vector.memset(pieces[:], 0.0)
+                    nc.vector.tensor_copy(out=pieces[:, :, 0], in_=ksum[:])
+                    nc.vector.tensor_sub(out=rest1[:], in0=ksum[:], in1=pieces[:, :, 0])
+                    nc.vector.tensor_copy(out=pieces[:, :, 1], in_=rest1[:])
+                    nc.vector.tensor_sub(out=rest2[:], in0=rest1[:], in1=pieces[:, :, 1])
+                    nc.vector.tensor_copy(out=pieces[:, :, 2], in_=rest2[:])
+                if c >= 1:
+                    cols = slice((c - 1) * 2 * E, c * 2 * E)
+                    nc.vector.quantize_mx(
+                        out=k_codes[:, cols].bitcast(FP8X4), scales=k_scales[:, cols], in_=k_grouped[c - 1][:]
                     )
-                    part = result[:, i * N_TILE : (i + 1) * N_TILE]
-                    if j % 3 == 1:
-                        nc.scalar.copy(out=part, in_=num[:])
-                        nc.gpsimd.tensor_mul(out=part, in0=part, in1=rden_all[:, n_cols])
-                    else:
-                        nc.vector.tensor_mul(out=part, in0=num[:], in1=rden_all[:, n_cols])
-                nc.sync.dma_start(out=out_rows[d_cols, s * STORE : (s + 1) * STORE], in_=result[:])
 
-        for m in range(D_TILES):
-            attend(m)
-            if m + AHEAD < D_TILES:
-                key_value_state(m + AHEAD)
+        staging = ctx.enter_context(tc.tile_pool(name="staging", bufs=4))
+        results = {}
+
+        def output_pass(m, j):
+            per_store = STORE // N_TILE
+            if j % per_store == 0:
+                results[m] = staging.tile([P, STORE], F32, tag="result", name="result")
+            d_cols = slice(m * P, (m + 1) * P)
+            n_cols = slice(j * N_TILE, (j + 1) * N_TILE)
+            num = new_bank([P, N_TILE])
+            nc.tensor.matmul_mx(
+                out=num[:],
+                lhsT=vk_codes[:, d_cols].bitcast(FP8X4),
+                lhsT_scale=vk_scales[:, d_cols],
+                rhs=q_codes[:, n_cols].bitcast(FP8X4),
+                rhs_scale=q_scales[:, n_cols],
+                start=True,
+                stop=True,
+            )
+            part = results[m][:, (j % per_store) * N_TILE : (j % per_store + 1) * N_TILE]
+            if j % 3 == 1:
+                nc.scalar.copy(out=part, in_=num[:])
+                nc.gpsimd.tensor_mul(out=part, in0=part, in1=rden_all[:, n_cols])
+            else:
+                nc.vector.tensor_mul(out=part, in0=num[:], in1=rden_all[:, n_cols])
+            if j % per_store == per_store - 1:
+                first = (j // per_store) * STORE
+                nc.sync.dma_start(out=out_rows[d_cols, first : first + STORE], in_=results[m][:])
+
+        def is_tile(m):
+            return 0 <= m < D_TILES
+
+        def is_range(r):
+            return 0 <= r < Q_RANGES
+
+        for p in range(-2, D_TILES):
+            if is_range(p - 1):
+                spread_den(p - 1)
+            if is_tile(p + 2):
+                transpose_v(p + 2)
+                if p + 2 + V_BUFS < D_TILES:
+                    load_v(p + 2 + V_BUFS)
+            if is_tile(p):
+                transpose_state(p)
+            if is_range(p):
+                regroup_q(p)
+            if is_range(p + 1):
+                relu_q(p + 1)
+            if is_tile(p):
+                quantise_state(p)
+            if is_range(p):
+                den_matmuls(p)
+            outputs = []
+            if p >= Q_RANGES:
+                first_tile = OUT_PER_ROUND * (p - Q_RANGES)
+                outputs = [(m, j) for m in range(first_tile, first_tile + OUT_PER_ROUND) for j in range(N_TILES)]
+            if is_tile(p + 1):
+                for g in range(TOKEN_PASSES):
+                    state_pass(p + 1, g)
+                    for m, j in outputs[OUT_PER_ROUND * g : OUT_PER_ROUND * (g + 1)]:
+                        output_pass(m, j)
+                round_state(p + 1)
+            else:
+                for m, j in outputs:
+                    output_pass(m, j)
+            if is_range(p):
+                reciprocal_den(p)
+            if is_tile(p + 2):
+                quantise_v(p + 2)
+            if is_range(p):
+                quantise_q(p)

@@ -32,6 +32,8 @@ STORE = 2048
 V_BUFS = 6
 BANKS = 6
 OUT_PER_ROUND = 2
+KSUM_PIECES = 3
+DEN_COLS = 32
 
 FLOPS = 2 * DV * E * N * 2 + 2 * E * N
 
@@ -68,7 +70,7 @@ def tile_relu_linear_att_pa_t_kernel(tc, q, k, v, out):
         rden_all = keep.tile([P, N], F32)
         ksum_parts = keep.tile([P, E_TILES, K_PIECES], F32)
         ksum = keep.tile([P, E_TILES], F32)
-        pieces = keep.tile([P, E_TILES, 4], BF16)
+        pieces = keep.tile([P, E_TILES, DEN_COLS], BF16)
         rest1 = keep.tile([P, E_TILES], F32)
         rest2 = keep.tile([P, E_TILES], F32)
         den = keep.tile([P, Q_RANGES, RANGE_TILES], F32)
@@ -172,7 +174,7 @@ def tile_relu_linear_att_pa_t_kernel(tc, q, k, v, out):
             nc.vector.quantize_mx(out=q_codes[:, cols].bitcast(FP8X4), scales=q_scales[:, cols], in_=q_grouped[r][:])
 
         def den_matmuls(r):
-            den_ps = new_bank([P, RANGE_TILES, 4])
+            den_ps = new_bank([P, RANGE_TILES, DEN_COLS])
             for j in range(RANGE_TILES):
                 for t in range(E_TILES):
                     nc.tensor.matmul(
@@ -185,7 +187,7 @@ def tile_relu_linear_att_pa_t_kernel(tc, q, k, v, out):
             den_sums[r] = den_ps
 
         def reciprocal_den(r):
-            nc.vector.tensor_reduce(out=den[:, r, :], in_=den_sums[r][:], axis=AXIS.X, op=ALU.add)
+            nc.vector.tensor_reduce(out=den[:, r, :], in_=den_sums[r][:, :, 0:KSUM_PIECES], axis=AXIS.X, op=ALU.add)
             nc.vector.reciprocal(out=rden[:, r, :], in_=den[:, r, :])
             rep = rep_pool.tile([P, RANGE_TILES, P], F32)
             nc.gpsimd.tensor_scalar(

@@ -22,16 +22,13 @@ E_TILES = E // P
 D_TILES = DV // P
 TOKEN_PASSES = N // K_PASS
 N_TILE = 512
-N_TILES = N // N_TILE
 K_PIECES = 4
 PIECE = N // K_PIECES
 Q_RANGES = 4
 RANGE = N // Q_RANGES
 RANGE_TILES = RANGE // P
-STORE = 2048
 V_BUFS = 6
 BANKS = 6
-OUT_PER_ROUND = 2
 KSUM_PIECES = 3
 DEN_COLS = 32
 
@@ -208,79 +205,51 @@ def tile_relu_linear_att_pa_t_kernel(tc, q, k, v, out):
                 first = r * RANGE + h * N_TILE
                 nc.scalar.copy(out=rden_all[:, first : first + N_TILE], in_=bank[:].rearrange("p i c -> p (i c)"))
 
-        with tc.tile_pool(name="k_in", bufs=K_PIECES) as k_in:
-            k_pieces = []
-            for c in range(K_PIECES):
-                piece = k_in.tile([P, E_TILES, PIECE], BF16, name="piece")
-                nc.sync.dma_start(
-                    out=piece[:],
-                    in_=k_rows.rearrange("(t p) n -> p t n", p=P)[:, :, c * PIECE : (c + 1) * PIECE],
+        k_pieces = {}
+        k_grouped = {}
+
+        def prepare_k(c):
+            kr = k_pieces[c]
+            grouped = grouped_pool.tile([P, PACK * 2 * E], BF16, tag="grouped", align_bytes=64)
+            grouped_words = grouped[:].bitcast(F32).rearrange("p (g e u) -> p g e u", g=2, u=2)
+            for t in range(E_TILES):
+                nc.vector.tensor_scalar(
+                    out=kr[:, t, :],
+                    in0=kr[:, t, :],
+                    scalar1=0.0,
+                    scalar2=None,
+                    op0=ALU.max,
+                    op1=ALU.add,
+                    accum_out=ksum_parts[:, t, c : c + 1],
                 )
-                k_pieces.append(piece)
-
-            def load_q(r):
-                nc.sync.dma_start(
-                    out=q_ranges[r][:],
-                    in_=q_rows.rearrange("(t p) n -> p t n", p=P)[:, :, r * RANGE : (r + 1) * RANGE],
+                bank = new_bank([P, 2, 2, P])
+                transpose_words(bank, kr[:, t, :].bitcast(F32), 0)
+                nc.scalar.copy(
+                    out=grouped_words[:, :, t * P : (t + 1) * P, :],
+                    in_=bank[:].rearrange("p g u e -> p g e u"),
                 )
+            k_grouped[c] = grouped
 
-            load_v(0)
-            load_v(1)
-            load_q(0)
-            load_q(1)
-            load_v(2)
-            load_q(2)
-            load_v(3)
-            load_q(3)
-            load_v(4)
-            load_v(5)
+        def quantise_k(c):
+            cols = slice(c * 2 * E, (c + 1) * 2 * E)
+            nc.vector.quantize_mx(out=k_codes[:, cols].bitcast(FP8X4), scales=k_scales[:, cols], in_=k_grouped[c][:])
 
-            k_grouped = {}
-            for c in range(K_PIECES + 1):
-                if c < K_PIECES:
-                    kr = k_pieces[c]
-                    grouped = grouped_pool.tile([P, PACK * 2 * E], BF16, tag="grouped", align_bytes=64)
-                    grouped_words = grouped[:].bitcast(F32).rearrange("p (g e u) -> p g e u", g=2, u=2)
-                    for t in range(E_TILES):
-                        nc.vector.tensor_scalar(
-                            out=kr[:, t, :],
-                            in0=kr[:, t, :],
-                            scalar1=0.0,
-                            scalar2=None,
-                            op0=ALU.max,
-                            op1=ALU.add,
-                            accum_out=ksum_parts[:, t, c : c + 1],
-                        )
-                        bank = new_bank([P, 2, 2, P])
-                        transpose_words(bank, kr[:, t, :].bitcast(F32), 0)
-                        nc.scalar.copy(
-                            out=grouped_words[:, :, t * P : (t + 1) * P, :],
-                            in_=bank[:].rearrange("p g u e -> p g e u"),
-                        )
-                    k_grouped[c] = grouped
-                if c == K_PIECES:
-                    nc.vector.tensor_reduce(out=ksum[:], in_=ksum_parts[:], axis=AXIS.X, op=ALU.add)
-                    nc.vector.memset(pieces[:], 0.0)
-                    nc.vector.tensor_copy(out=pieces[:, :, 0], in_=ksum[:])
-                    nc.vector.tensor_sub(out=rest1[:], in0=ksum[:], in1=pieces[:, :, 0])
-                    nc.vector.tensor_copy(out=pieces[:, :, 1], in_=rest1[:])
-                    nc.vector.tensor_sub(out=rest2[:], in0=rest1[:], in1=pieces[:, :, 1])
-                    nc.vector.tensor_copy(out=pieces[:, :, 2], in_=rest2[:])
-                if c >= 1:
-                    cols = slice((c - 1) * 2 * E, c * 2 * E)
-                    nc.vector.quantize_mx(
-                        out=k_codes[:, cols].bitcast(FP8X4), scales=k_scales[:, cols], in_=k_grouped[c - 1][:]
-                    )
+        def split_ksum():
+            nc.vector.tensor_reduce(out=ksum[:], in_=ksum_parts[:], axis=AXIS.X, op=ALU.add)
+            nc.vector.memset(pieces[:], 0.0)
+            nc.vector.tensor_copy(out=pieces[:, :, 0], in_=ksum[:])
+            nc.vector.tensor_sub(out=rest1[:], in0=ksum[:], in1=pieces[:, :, 0])
+            nc.vector.tensor_copy(out=pieces[:, :, 1], in_=rest1[:])
+            nc.vector.tensor_sub(out=rest2[:], in0=rest1[:], in1=pieces[:, :, 1])
+            nc.vector.tensor_copy(out=pieces[:, :, 2], in_=rest2[:])
 
-        staging = ctx.enter_context(tc.tile_pool(name="staging", bufs=4))
         results = {}
 
-        def output_pass(m, j):
-            per_store = STORE // N_TILE
-            if j % per_store == 0:
-                results[m] = staging.tile([P, STORE], F32, tag="result", name="result")
+        def output_pass(m, r, h):
+            if h == 0:
+                results[(m, r)] = staging.tile([P, RANGE], F32, tag="result", name="result")
             d_cols = slice(m * P, (m + 1) * P)
-            n_cols = slice(j * N_TILE, (j + 1) * N_TILE)
+            n_cols = slice(r * RANGE + h * N_TILE, r * RANGE + (h + 1) * N_TILE)
             num = new_bank([P, N_TILE])
             nc.tensor.matmul_mx(
                 out=num[:],
@@ -291,15 +260,17 @@ def tile_relu_linear_att_pa_t_kernel(tc, q, k, v, out):
                 start=True,
                 stop=True,
             )
-            part = results[m][:, (j % per_store) * N_TILE : (j % per_store + 1) * N_TILE]
-            if j % 3 == 1:
+            part = results[(m, r)][:, h * N_TILE : (h + 1) * N_TILE]
+            if (2 * (m + r) + h) % 3 == 1:
                 nc.scalar.copy(out=part, in_=num[:])
                 nc.gpsimd.tensor_mul(out=part, in0=part, in1=rden_all[:, n_cols])
             else:
                 nc.vector.tensor_mul(out=part, in0=num[:], in1=rden_all[:, n_cols])
-            if j % per_store == per_store - 1:
-                first = (j // per_store) * STORE
-                nc.sync.dma_start(out=out_rows[d_cols, first : first + STORE], in_=results[m][:])
+            if h == RANGE // N_TILE - 1:
+                nc.sync.dma_start(out=out_rows[d_cols, r * RANGE : (r + 1) * RANGE], in_=results[(m, r)][:])
+
+        def is_piece(c):
+            return 0 <= c < K_PIECES
 
         def is_tile(m):
             return 0 <= m < D_TILES
@@ -307,15 +278,25 @@ def tile_relu_linear_att_pa_t_kernel(tc, q, k, v, out):
         def is_range(r):
             return 0 <= r < Q_RANGES
 
-        for p in range(-2, D_TILES):
-            if is_range(p - 1):
-                spread_den(p - 1)
+        def work_round(p):
+            if is_piece(p + K_PIECES):
+                prepare_k(p + K_PIECES)
+            if is_piece(p + K_PIECES - 1) and p < 0:
+                quantise_k(p + K_PIECES - 1)
             if is_tile(p + 2):
                 transpose_v(p + 2)
                 if p + 2 + V_BUFS < D_TILES:
                     load_v(p + 2 + V_BUFS)
+            if is_range(p - 1):
+                spread_den(p - 1)
             if is_tile(p):
                 transpose_state(p)
+            if is_tile(p + 1):
+                quantise_v(p + 1)
+            if p == -1:
+                quantise_k(K_PIECES - 1)
+            if p == 0:
+                split_ksum()
             if is_range(p):
                 regroup_q(p)
             if is_range(p + 1):
@@ -324,22 +305,51 @@ def tile_relu_linear_att_pa_t_kernel(tc, q, k, v, out):
                 quantise_state(p)
             if is_range(p):
                 den_matmuls(p)
-            outputs = []
-            if p >= Q_RANGES:
-                first_tile = OUT_PER_ROUND * (p - Q_RANGES)
-                outputs = [(m, j) for m in range(first_tile, first_tile + OUT_PER_ROUND) for j in range(N_TILES)]
+                reciprocal_den(p)
+            blocks = []
+            if is_range(p - 1):
+                blocks = blocks + [(m, p - 1) for m in range(p - 1)]
+            if is_tile(p - 1):
+                blocks = blocks + [(p - 1, r) for r in range(min(p, Q_RANGES))]
+            passes = [(m, r, h) for m, r in blocks for h in range(RANGE // N_TILE)]
+            share = (len(passes) + TOKEN_PASSES - 1) // TOKEN_PASSES
             if is_tile(p + 1):
                 for g in range(TOKEN_PASSES):
                     state_pass(p + 1, g)
-                    for m, j in outputs[OUT_PER_ROUND * g : OUT_PER_ROUND * (g + 1)]:
-                        output_pass(m, j)
+                    for m, r, h in passes[share * g : share * (g + 1)]:
+                        output_pass(m, r, h)
                 round_state(p + 1)
             else:
-                for m, j in outputs:
-                    output_pass(m, j)
-            if is_range(p):
-                reciprocal_den(p)
-            if is_tile(p + 2):
-                quantise_v(p + 2)
+                for m, r, h in passes:
+                    output_pass(m, r, h)
             if is_range(p):
                 quantise_q(p)
+
+        def load_q(r):
+            nc.sync.dma_start(
+                out=q_ranges[r][:],
+                in_=q_rows.rearrange("(t p) n -> p t n", p=P)[:, :, r * RANGE : (r + 1) * RANGE],
+            )
+
+        with tc.tile_pool(name="k_in", bufs=K_PIECES) as k_in:
+            for c in range(K_PIECES):
+                k_pieces[c] = k_in.tile([P, E_TILES, PIECE], BF16, name="piece")
+                for t in range(E_TILES):
+                    nc.sync.dma_start(
+                        out=k_pieces[c][:, t, :], in_=k_rows[t * P : (t + 1) * P, c * PIECE : (c + 1) * PIECE]
+                    )
+            load_v(0)
+            load_v(1)
+            load_q(0)
+            load_q(1)
+            load_v(2)
+            load_q(2)
+            load_v(3)
+            load_q(3)
+            load_v(4)
+            load_v(5)
+            for p in range(-K_PIECES, 0):
+                work_round(p)
+        staging = ctx.enter_context(tc.tile_pool(name="staging", bufs=8))
+        for p in range(0, D_TILES + 1):
+            work_round(p)

@@ -28,7 +28,9 @@ Q_RANGES = 4
 RANGE = N // Q_RANGES
 RANGE_TILES = RANGE // P
 V_BUFS = 6
-BANKS = 6
+BANKS = 7
+STATE_PASSES = E_TILES * TOKEN_PASSES
+STEPS = 8
 KSUM_PIECES = 3
 DEN_COLS = 32
 
@@ -54,8 +56,6 @@ def tile_relu_linear_att_pa_t_kernel(tc, q, k, v, out):
 
         ident_f32 = keep.tile([P, P], F32)
         make_identity(nc, ident_f32[:])
-        ident_bf16 = keep.tile([P, P], BF16)
-        make_identity(nc, ident_bf16[:])
 
         k_codes = keep.tile([P, TOKEN_PASSES * E], U32, align_bytes=64)
         k_scales = keep.tile([P, TOKEN_PASSES * E], U8, align_bytes=64)
@@ -87,7 +87,6 @@ def tile_relu_linear_att_pa_t_kernel(tc, q, k, v, out):
         v_quantised = {}
         vk_sums = {}
         vk_rounded = {}
-        vk_turned = {}
 
         def load_v(m):
             v_sb = v_in.tile([P, N], BF16, name="v_sb")
@@ -112,39 +111,34 @@ def tile_relu_linear_att_pa_t_kernel(tc, q, k, v, out):
             nc.vector.quantize_mx(out=codes[:].bitcast(FP8X4), scales=scales[:], in_=v_grouped[m][:])
             v_quantised[m] = (codes, scales)
 
-        def state_pass(m, g):
-            if g == 0:
-                vk_sums[m] = psum.tile([P, E], F32, tag="vk_ps", bufs=1, name="vk_ps")
+        def state_pass(m, i):
+            t = i // TOKEN_PASSES
+            g = i % TOKEN_PASSES
+            if i == 0:
+                vk_sums[m] = psum.tile([P, E_TILES, P], F32, tag="vk_ps", bufs=1, name="vk_ps")
             codes, scales = v_quantised[m]
+            e_cols = slice(g * E + t * P, g * E + (t + 1) * P)
             nc.tensor.matmul_mx(
-                out=vk_sums[m][:],
-                lhsT=codes[:, g * P : (g + 1) * P].bitcast(FP8X4),
-                lhsT_scale=scales[:, g * P : (g + 1) * P],
-                rhs=k_codes[:, g * E : (g + 1) * E].bitcast(FP8X4),
-                rhs_scale=k_scales[:, g * E : (g + 1) * E],
+                out=vk_sums[m][:, t, :],
+                lhsT=k_codes[:, e_cols].bitcast(FP8X4),
+                lhsT_scale=k_scales[:, e_cols],
+                rhs=codes[:, g * P : (g + 1) * P].bitcast(FP8X4),
+                rhs_scale=scales[:, g * P : (g + 1) * P],
                 start=(g == 0),
                 stop=(g == TOKEN_PASSES - 1),
             )
 
         def round_state(m):
-            vk_bf = vk_pool.tile([P, E], BF16, tag="vk_bf")
-            nc.scalar.copy(out=vk_bf[:], in_=vk_sums[m][:])
-            vk_rounded[m] = vk_bf
-
-        def transpose_state(m):
-            vk_t = psum.tile([P, E_TILES, P], BF16, tag="vk_t", bufs=1)
-            for t in range(E_TILES):
-                nc.tensor.transpose(vk_t[:, t, :], vk_rounded[m][:, t * P : (t + 1) * P], ident_bf16[:])
-            vk_turned[m] = vk_t
+            vk_grouped = vk_pool.tile([P, P, PACK], BF16, tag="vk_grouped", align_bytes=64)
+            nc.scalar.copy(out=vk_grouped[:], in_=vk_sums[m][:].rearrange("p t d -> p d t"))
+            vk_rounded[m] = vk_grouped
 
         def quantise_state(m):
-            vk_grouped = vk_pool.tile([P, P, PACK], BF16, tag="vk_grouped", align_bytes=64)
-            nc.vector.tensor_copy(out=vk_grouped[:], in_=vk_turned[m][:].rearrange("p t d -> p d t"))
             cols = slice(m * P, (m + 1) * P)
             nc.vector.quantize_mx(
                 out=vk_codes[:, cols].bitcast(FP8X4),
                 scales=vk_scales[:, cols],
-                in_=vk_grouped[:].rearrange("p d t -> p (d t)"),
+                in_=vk_rounded[m][:].rearrange("p d t -> p (d t)"),
             )
 
         q_grouped = {}
@@ -289,10 +283,8 @@ def tile_relu_linear_att_pa_t_kernel(tc, q, k, v, out):
                     load_v(p + 2 + V_BUFS)
             if is_range(p - 1):
                 spread_den(p - 1)
-            if is_tile(p):
-                transpose_state(p)
-            if is_tile(p + 1):
-                quantise_v(p + 1)
+            if p + 1 == 0:
+                quantise_v(0)
             if p == -1:
                 quantise_k(K_PIECES - 1)
             if p == 0:
@@ -312,12 +304,15 @@ def tile_relu_linear_att_pa_t_kernel(tc, q, k, v, out):
             if is_tile(p - 1):
                 blocks = blocks + [(p - 1, r) for r in range(min(p, Q_RANGES))]
             passes = [(m, r, h) for m, r in blocks for h in range(RANGE // N_TILE)]
-            share = (len(passes) + TOKEN_PASSES - 1) // TOKEN_PASSES
+            share = (len(passes) + STEPS - 1) // STEPS
             if is_tile(p + 1):
-                for g in range(TOKEN_PASSES):
-                    state_pass(p + 1, g)
-                    for m, r, h in passes[share * g : share * (g + 1)]:
+                for s in range(STEPS):
+                    for i in range(s * STATE_PASSES // STEPS, (s + 1) * STATE_PASSES // STEPS):
+                        state_pass(p + 1, i)
+                    for m, r, h in passes[share * s : share * (s + 1)]:
                         output_pass(m, r, h)
+                    if s == STEPS // 2 - 1 and is_tile(p + 2):
+                        quantise_v(p + 2)
                 round_state(p + 1)
             else:
                 for m, r, h in passes:

@@ -45,7 +45,6 @@ def tile_relu_linear_att_pa_t_kernel(tc, q, k, v, out):
     out_rows = out.rearrange("b (d x) c -> (b d) (x c)", x=N // DV)
 
     with ExitStack() as ctx:
-        ctx.enter_context(tc.manual_schedule())
         keep = ctx.enter_context(tc.tile_pool(name="keep", bufs=1))
         v_in = ctx.enter_context(tc.tile_pool(name="v_in", bufs=V_BUFS))
         grouped_pool = ctx.enter_context(tc.tile_pool(name="grouped", bufs=3))

@@ -8,7 +8,6 @@ BF16 = mybir.dt.bfloat16
 U32 = mybir.dt.uint32
 U8 = mybir.dt.uint8
 FP8X4 = mybir.dt.float8_e4m3fn_x4
-ACT = mybir.ActivationFunctionType
 ALU = mybir.AluOpType
 AXIS = mybir.AxisListType
 
@@ -21,18 +20,33 @@ N = 4096
 E_TILES = E // P
 D_TILES = DV // P
 TOKEN_PASSES = N // K_PASS
+PAIR = 2
+PASS_WORDS = K_PASS // PAIR
+BANK_PASSES = 2
 N_TILE = 512
-K_PIECES = 4
-PIECE = N // K_PIECES
+K_PARTS = 2
+K_PART = N // K_PARTS
 Q_RANGES = 4
 RANGE = N // Q_RANGES
 RANGE_TILES = RANGE // P
-V_BUFS = 6
-BANKS = 7
+RANGE_BANKS = RANGE // N_TILE
+RUN = 4
 STATE_PASSES = E_TILES * TOKEN_PASSES
 STEPS = 8
 KSUM_PIECES = 3
 DEN_COLS = 32
+
+V_BUFS = 6
+GROUPED_BUFS = 3
+V_MX_BUFS = 2
+VK_BUFS = 2
+REP_BUFS = 2
+BANKS = 7
+STAGING_BUFS = 8
+
+FIRST_ROUND = -E_TILES
+FIRST_STATE_ROUND = -1
+LAST_ROUND = D_TILES
 
 FLOPS = 2 * DV * E * N * 2 + 2 * E * N
 
@@ -45,12 +59,13 @@ def tile_relu_linear_att_pa_t_kernel(tc, q, k, v, out):
     out_rows = out.rearrange("b (d x) c -> (b d) (x c)", x=N // DV)
 
     with ExitStack() as ctx:
+        ctx.enter_context(tc.manual_schedule())
         keep = ctx.enter_context(tc.tile_pool(name="keep", bufs=1))
         v_in = ctx.enter_context(tc.tile_pool(name="v_in", bufs=V_BUFS))
-        grouped_pool = ctx.enter_context(tc.tile_pool(name="grouped", bufs=3))
-        v_mx = ctx.enter_context(tc.tile_pool(name="v_mx", bufs=2))
-        vk_pool = ctx.enter_context(tc.tile_pool(name="vk", bufs=2))
-        rep_pool = ctx.enter_context(tc.tile_pool(name="rep", bufs=2))
+        grouped_pool = ctx.enter_context(tc.tile_pool(name="grouped", bufs=GROUPED_BUFS))
+        v_mx = ctx.enter_context(tc.tile_pool(name="v_mx", bufs=V_MX_BUFS))
+        vk_pool = ctx.enter_context(tc.tile_pool(name="vk", bufs=VK_BUFS))
+        rep_pool = ctx.enter_context(tc.tile_pool(name="rep", bufs=REP_BUFS))
         psum = ctx.enter_context(tc.psum_pool(name="psum", bufs=1))
 
         ident_f32 = keep.tile([P, P], F32)
@@ -64,7 +79,7 @@ def tile_relu_linear_att_pa_t_kernel(tc, q, k, v, out):
         vk_scales = keep.tile([P, DV], U8, align_bytes=64)
         q_ranges = [keep.tile([P, E_TILES, RANGE], BF16, name="q_sb%d" % r) for r in range(Q_RANGES)]
         rden_all = keep.tile([P, N], F32)
-        ksum_parts = keep.tile([P, E_TILES, K_PIECES], F32)
+        ksum_parts = keep.tile([P, E_TILES, K_PARTS], F32)
         ksum = keep.tile([P, E_TILES], F32)
         pieces = keep.tile([P, E_TILES, DEN_COLS], BF16)
         rest1 = keep.tile([P, E_TILES], F32)
@@ -75,11 +90,21 @@ def tile_relu_linear_att_pa_t_kernel(tc, q, k, v, out):
         def new_bank(shape):
             return psum.tile(shape, F32, tag="bank", bufs=BANKS, name="bank")
 
-        def transpose_words(bank, words, first_word):
-            for g in range(2):
-                for u in range(2):
-                    w0 = first_word + (2 * g + u) * P
-                    nc.tensor.transpose(bank[:, g, u, :], words[:, w0 : w0 + P], ident_f32[:])
+        def tokens_to_partitions(rows):
+            words = rows[:].bitcast(F32)
+            grouped = grouped_pool.tile([P, PACK * TOKEN_PASSES * P], BF16, tag="grouped", align_bytes=64)
+            grouped_words = grouped[:].bitcast(F32).rearrange("p (g d u) -> p g d u", g=TOKEN_PASSES, u=PAIR)
+            for first_pass in range(0, TOKEN_PASSES, BANK_PASSES):
+                bank = new_bank([P, BANK_PASSES, PAIR, P])
+                for g in range(BANK_PASSES):
+                    for u in range(PAIR):
+                        w0 = (first_pass + g) * PASS_WORDS + u * P
+                        nc.tensor.transpose(bank[:, g, u, :], words[:, w0 : w0 + P], ident_f32[:])
+                nc.scalar.copy(
+                    out=grouped_words[:, first_pass : first_pass + BANK_PASSES, :, :],
+                    in_=bank[:].rearrange("p g u d -> p g d u"),
+                )
+            return grouped
 
         v_tiles = {}
         v_grouped = {}
@@ -93,16 +118,7 @@ def tile_relu_linear_att_pa_t_kernel(tc, q, k, v, out):
             v_tiles[m] = v_sb
 
         def transpose_v(m):
-            words = v_tiles[m][:].bitcast(F32)
-            grouped = grouped_pool.tile([P, PACK * TOKEN_PASSES * P], BF16, tag="grouped", align_bytes=64)
-            grouped_words = grouped[:].bitcast(F32).rearrange("p (g d u) -> p g d u", g=TOKEN_PASSES, u=2)
-            for b in range(TOKEN_PASSES // 2):
-                bank = new_bank([P, 2, 2, P])
-                transpose_words(bank, words, 2 * b * (K_PASS // 2))
-                nc.scalar.copy(
-                    out=grouped_words[:, 2 * b : 2 * b + 2, :, :], in_=bank[:].rearrange("p g u d -> p g d u")
-                )
-            v_grouped[m] = grouped
+            v_grouped[m] = tokens_to_partitions(v_tiles[m])
 
         def quantise_v(m):
             codes = v_mx.tile([P, TOKEN_PASSES * P], U32, tag="v_codes", align_bytes=64)
@@ -116,7 +132,7 @@ def tile_relu_linear_att_pa_t_kernel(tc, q, k, v, out):
             if i == 0:
                 vk_sums[m] = psum.tile([P, E_TILES, P], F32, tag="vk_ps", bufs=1, name="vk_ps")
             codes, scales = v_quantised[m]
-            e_cols = slice(g * E + t * P, g * E + (t + 1) * P)
+            e_cols = slice((t * TOKEN_PASSES + g) * P, (t * TOKEN_PASSES + g + 1) * P)
             nc.tensor.matmul_mx(
                 out=vk_sums[m][:, t, :],
                 lhsT=k_codes[:, e_cols].bitcast(FP8X4),
@@ -144,16 +160,24 @@ def tile_relu_linear_att_pa_t_kernel(tc, q, k, v, out):
         den_sums = {}
         repeated = {}
 
+        def load_q(r):
+            nc.sync.dma_start(
+                out=q_ranges[r][:],
+                in_=q_rows.rearrange("(t p) n -> p t n", p=P)[:, :, r * RANGE : (r + 1) * RANGE],
+            )
+
         def relu_q(r):
             nc.vector.tensor_scalar_max(out=q_ranges[r][:], in0=q_ranges[r][:], scalar1=0.0)
 
         def regroup_q(r):
             grouped = grouped_pool.tile([P, PACK * RANGE], BF16, tag="grouped", align_bytes=64)
             half = RANGE // 2
-            for s in range(2):
-                dst = grouped[:, s * PACK * half : (s + 1) * PACK * half].rearrange("p (c i t) -> p c t i", i=4, t=PACK)
-                src = q_ranges[r][:, :, s * half : (s + 1) * half].rearrange("p t (c i) -> p c t i", i=4)
-                if s == 0:
+            for side in range(2):
+                dst = grouped[:, side * PACK * half : (side + 1) * PACK * half].rearrange(
+                    "p (c i t) -> p c t i", i=RUN, t=PACK
+                )
+                src = q_ranges[r][:, :, side * half : (side + 1) * half].rearrange("p t (c i) -> p c t i", i=RUN)
+                if side == 0:
                     nc.vector.tensor_copy(out=dst, in_=src)
                 else:
                     nc.scalar.copy(out=dst, in_=src)
@@ -191,41 +215,35 @@ def tile_relu_linear_att_pa_t_kernel(tc, q, k, v, out):
             repeated[r] = rep
 
         def spread_den(r):
-            for h in range(RANGE // N_TILE):
+            for h in range(RANGE_BANKS):
                 bank = new_bank([P, N_TILE // P, P])
-                for i in range(N_TILE // P):
-                    nc.tensor.transpose(bank[:, i, :], repeated[r][:, h * (N_TILE // P) + i, :], ident_f32[:])
+                for square in range(N_TILE // P):
+                    nc.tensor.transpose(
+                        bank[:, square, :], repeated[r][:, h * (N_TILE // P) + square, :], ident_f32[:]
+                    )
                 first = r * RANGE + h * N_TILE
                 nc.scalar.copy(out=rden_all[:, first : first + N_TILE], in_=bank[:].rearrange("p i c -> p (i c)"))
 
-        k_pieces = {}
+        k_tiles = {}
         k_grouped = {}
 
-        def prepare_k(c):
-            kr = k_pieces[c]
-            grouped = grouped_pool.tile([P, PACK * 2 * E], BF16, tag="grouped", align_bytes=64)
-            grouped_words = grouped[:].bitcast(F32).rearrange("p (g e u) -> p g e u", g=2, u=2)
-            for t in range(E_TILES):
+        def prepare_k(t):
+            kr = k_tiles[t]
+            for c in range(K_PARTS):
                 nc.vector.tensor_scalar(
-                    out=kr[:, t, :],
-                    in0=kr[:, t, :],
+                    out=kr[:, c * K_PART : (c + 1) * K_PART],
+                    in0=kr[:, c * K_PART : (c + 1) * K_PART],
                     scalar1=0.0,
                     scalar2=None,
                     op0=ALU.max,
                     op1=ALU.add,
                     accum_out=ksum_parts[:, t, c : c + 1],
                 )
-                bank = new_bank([P, 2, 2, P])
-                transpose_words(bank, kr[:, t, :].bitcast(F32), 0)
-                nc.scalar.copy(
-                    out=grouped_words[:, :, t * P : (t + 1) * P, :],
-                    in_=bank[:].rearrange("p g u e -> p g e u"),
-                )
-            k_grouped[c] = grouped
+            k_grouped[t] = tokens_to_partitions(kr)
 
-        def quantise_k(c):
-            cols = slice(c * 2 * E, (c + 1) * 2 * E)
-            nc.vector.quantize_mx(out=k_codes[:, cols].bitcast(FP8X4), scales=k_scales[:, cols], in_=k_grouped[c][:])
+        def quantise_k(t):
+            cols = slice(t * TOKEN_PASSES * P, (t + 1) * TOKEN_PASSES * P)
+            nc.vector.quantize_mx(out=k_codes[:, cols].bitcast(FP8X4), scales=k_scales[:, cols], in_=k_grouped[t][:])
 
         def split_ksum():
             nc.vector.tensor_reduce(out=ksum[:], in_=ksum_parts[:], axis=AXIS.X, op=ALU.add)
@@ -254,16 +272,16 @@ def tile_relu_linear_att_pa_t_kernel(tc, q, k, v, out):
                 stop=True,
             )
             part = results[(m, r)][:, h * N_TILE : (h + 1) * N_TILE]
-            if (2 * (m + r) + h) % 3 == 1:
+            if (RANGE_BANKS * (m + r) + h) % 3 == 1:
                 nc.scalar.copy(out=part, in_=num[:])
                 nc.gpsimd.tensor_mul(out=part, in0=part, in1=rden_all[:, n_cols])
             else:
                 nc.vector.tensor_mul(out=part, in0=num[:], in1=rden_all[:, n_cols])
-            if h == RANGE // N_TILE - 1:
+            if h == RANGE_BANKS - 1:
                 nc.sync.dma_start(out=out_rows[d_cols, r * RANGE : (r + 1) * RANGE], in_=results[(m, r)][:])
 
-        def is_piece(c):
-            return 0 <= c < K_PIECES
+        def is_k_tile(t):
+            return 0 <= t < E_TILES
 
         def is_tile(m):
             return 0 <= m < D_TILES
@@ -272,21 +290,20 @@ def tile_relu_linear_att_pa_t_kernel(tc, q, k, v, out):
             return 0 <= r < Q_RANGES
 
         def work_round(p):
-            if is_piece(p + K_PIECES):
-                prepare_k(p + K_PIECES)
-            if is_piece(p + K_PIECES - 1) and p < 0:
-                quantise_k(p + K_PIECES - 1)
+            if is_k_tile(p + E_TILES):
+                prepare_k(p + E_TILES)
+            if is_k_tile(p + E_TILES - 1) and p + E_TILES - 1 != E_TILES - 1:
+                quantise_k(p + E_TILES - 1)
             if is_tile(p + 2):
                 transpose_v(p + 2)
                 if p + 2 + V_BUFS < D_TILES:
                     load_v(p + 2 + V_BUFS)
             if is_range(p - 1):
                 spread_den(p - 1)
-            if p + 1 == 0:
+            if p == FIRST_STATE_ROUND:
                 quantise_v(0)
-            if p == -1:
-                quantise_k(K_PIECES - 1)
-            if p == 0:
+                quantise_k(E_TILES - 1)
+            if p == FIRST_STATE_ROUND + 1:
                 split_ksum()
             if is_range(p):
                 regroup_q(p)
@@ -302,7 +319,7 @@ def tile_relu_linear_att_pa_t_kernel(tc, q, k, v, out):
                 blocks = blocks + [(m, p - 1) for m in range(p - 1)]
             if is_tile(p - 1):
                 blocks = blocks + [(p - 1, r) for r in range(min(p, Q_RANGES))]
-            passes = [(m, r, h) for m, r in blocks for h in range(RANGE // N_TILE)]
+            passes = [(m, r, h) for m, r in blocks for h in range(RANGE_BANKS)]
             share = (len(passes) + STEPS - 1) // STEPS
             if is_tile(p + 1):
                 for s in range(STEPS):
@@ -319,31 +336,24 @@ def tile_relu_linear_att_pa_t_kernel(tc, q, k, v, out):
             if is_range(p):
                 quantise_q(p)
 
-        def load_q(r):
-            nc.sync.dma_start(
-                out=q_ranges[r][:],
-                in_=q_rows.rearrange("(t p) n -> p t n", p=P)[:, :, r * RANGE : (r + 1) * RANGE],
-            )
-
-        with tc.tile_pool(name="k_in", bufs=K_PIECES) as k_in:
-            for c in range(K_PIECES):
-                k_pieces[c] = k_in.tile([P, E_TILES, PIECE], BF16, name="piece")
-                for t in range(E_TILES):
+        with tc.tile_pool(name="k_in", bufs=E_TILES) as k_in:
+            for t in range(E_TILES):
+                k_tiles[t] = k_in.tile([P, N], BF16, name="k_sb")
+                for c in range(K_PARTS):
                     nc.sync.dma_start(
-                        out=k_pieces[c][:, t, :], in_=k_rows[t * P : (t + 1) * P, c * PIECE : (c + 1) * PIECE]
+                        out=k_tiles[t][:, c * K_PART : (c + 1) * K_PART],
+                        in_=k_rows[t * P : (t + 1) * P, c * K_PART : (c + 1) * K_PART],
                     )
             load_v(0)
             load_v(1)
             load_q(0)
-            load_q(1)
-            load_v(2)
-            load_q(2)
-            load_v(3)
-            load_q(3)
-            load_v(4)
-            load_v(5)
-            for p in range(-K_PIECES, 0):
+            for r in range(1, Q_RANGES):
+                load_q(r)
+                load_v(r + 1)
+            for m in range(Q_RANGES + 1, V_BUFS):
+                load_v(m)
+            for p in range(FIRST_ROUND, 0):
                 work_round(p)
-        staging = ctx.enter_context(tc.tile_pool(name="staging", bufs=8))
-        for p in range(0, D_TILES + 1):
+        staging = ctx.enter_context(tc.tile_pool(name="staging", bufs=STAGING_BUFS))
+        for p in range(0, LAST_ROUND + 1):
             work_round(p)

from contextlib import ExitStack

import concourse.mybir as mybir
from concourse.masks import make_identity

F32 = mybir.dt.float32
BF16 = mybir.dt.bfloat16
U32 = mybir.dt.uint32
U8 = mybir.dt.uint8
FP8X4 = mybir.dt.float8_e4m3fn_x4
ALU = mybir.AluOpType
AXIS = mybir.AxisListType

P = 128
PACK = 4
K_PASS = P * PACK
E = 512
DV = 1024
N = 4096
E_TILES = E // P
D_TILES = DV // P
TOKEN_PASSES = N // K_PASS
PAIR = 2
PASS_WORDS = K_PASS // PAIR
BANK_PASSES = 2
N_TILE = 512
K_PARTS = 2
K_PART = N // K_PARTS
Q_RANGES = 4
RANGE = N // Q_RANGES
RANGE_TILES = RANGE // P
RANGE_BANKS = RANGE // N_TILE
RUN = 4
STATE_PASSES = E_TILES * TOKEN_PASSES
STEPS = 8
KSUM_PIECES = 3
DEN_COLS = 32

V_BUFS = 6
GROUPED_BUFS = 3
V_MX_BUFS = 2
VK_BUFS = 2
REP_BUFS = 2
BANKS = 7
STAGING_BUFS = 8

FIRST_ROUND = -E_TILES
FIRST_STATE_ROUND = -1
LAST_ROUND = D_TILES

FLOPS = 2 * DV * E * N * 2 + 2 * E * N


def tile_relu_linear_att_pa_t_kernel(tc, q, k, v, out):
    nc = tc.nc
    q_rows = q.rearrange("b h e n -> (b h e) n")
    k_rows = k.rearrange("b h e n -> (b h e) n")
    v_rows = v.rearrange("b h d n -> (b h d) n")
    out_rows = out.rearrange("b (d x) c -> (b d) (x c)", x=N // DV)

    with ExitStack() as ctx:
        ctx.enter_context(tc.manual_schedule())
        keep = ctx.enter_context(tc.tile_pool(name="keep", bufs=1))
        v_in = ctx.enter_context(tc.tile_pool(name="v_in", bufs=V_BUFS))
        grouped_pool = ctx.enter_context(tc.tile_pool(name="grouped", bufs=GROUPED_BUFS))
        v_mx = ctx.enter_context(tc.tile_pool(name="v_mx", bufs=V_MX_BUFS))
        vk_pool = ctx.enter_context(tc.tile_pool(name="vk", bufs=VK_BUFS))
        rep_pool = ctx.enter_context(tc.tile_pool(name="rep", bufs=REP_BUFS))
        psum = ctx.enter_context(tc.psum_pool(name="psum", bufs=1))

        ident_f32 = keep.tile([P, P], F32)
        make_identity(nc, ident_f32[:])

        k_codes = keep.tile([P, TOKEN_PASSES * E], U32, align_bytes=64)
        k_scales = keep.tile([P, TOKEN_PASSES * E], U8, align_bytes=64)
        q_codes = keep.tile([P, N], U32, align_bytes=64)
        q_scales = keep.tile([P, N], U8, align_bytes=64)
        vk_codes = keep.tile([P, DV], U32, align_bytes=64)
        vk_scales = keep.tile([P, DV], U8, align_bytes=64)
        q_ranges = [keep.tile([P, E_TILES, RANGE], BF16, name="q_sb%d" % r) for r in range(Q_RANGES)]
        rden_all = keep.tile([P, N], F32)
        ksum_parts = keep.tile([P, E_TILES, K_PARTS], F32)
        ksum = keep.tile([P, E_TILES], F32)
        pieces = keep.tile([P, E_TILES, DEN_COLS], BF16)
        rest1 = keep.tile([P, E_TILES], F32)
        rest2 = keep.tile([P, E_TILES], F32)
        den = keep.tile([P, Q_RANGES, RANGE_TILES], F32)
        rden = keep.tile([P, Q_RANGES, RANGE_TILES], F32)

        def new_bank(shape):
            return psum.tile(shape, F32, tag="bank", bufs=BANKS, name="bank")

        def tokens_to_partitions(rows):
            words = rows[:].bitcast(F32)
            grouped = grouped_pool.tile([P, PACK * TOKEN_PASSES * P], BF16, tag="grouped", align_bytes=64)
            grouped_words = grouped[:].bitcast(F32).rearrange("p (g d u) -> p g d u", g=TOKEN_PASSES, u=PAIR)
            for first_pass in range(0, TOKEN_PASSES, BANK_PASSES):
                bank = new_bank([P, BANK_PASSES, PAIR, P])
                for g in range(BANK_PASSES):
                    for u in range(PAIR):
                        w0 = (first_pass + g) * PASS_WORDS + u * P
                        nc.tensor.transpose(bank[:, g, u, :], words[:, w0 : w0 + P], ident_f32[:])
                nc.scalar.copy(
                    out=grouped_words[:, first_pass : first_pass + BANK_PASSES, :, :],
                    in_=bank[:].rearrange("p g u d -> p g d u"),
                )
            return grouped

        v_tiles = {}
        v_grouped = {}
        v_quantised = {}
        vk_sums = {}
        vk_rounded = {}

        def load_v(m):
            v_sb = v_in.tile([P, N], BF16, name="v_sb")
            nc.sync.dma_start(out=v_sb[:], in_=v_rows[m * P : (m + 1) * P, :])
            v_tiles[m] = v_sb

        def transpose_v(m):
            v_grouped[m] = tokens_to_partitions(v_tiles[m])

        def quantise_v(m):
            codes = v_mx.tile([P, TOKEN_PASSES * P], U32, tag="v_codes", align_bytes=64)
            scales = v_mx.tile([P, TOKEN_PASSES * P], U8, tag="v_scales", align_bytes=64)
            nc.vector.quantize_mx(out=codes[:].bitcast(FP8X4), scales=scales[:], in_=v_grouped[m][:])
            v_quantised[m] = (codes, scales)

        def state_pass(m, i):
            t = i // TOKEN_PASSES
            g = i % TOKEN_PASSES
            if i == 0:
                vk_sums[m] = psum.tile([P, E_TILES, P], F32, tag="vk_ps", bufs=1, name="vk_ps")
            codes, scales = v_quantised[m]
            e_cols = slice((t * TOKEN_PASSES + g) * P, (t * TOKEN_PASSES + g + 1) * P)
            nc.tensor.matmul_mx(
                out=vk_sums[m][:, t, :],
                lhsT=k_codes[:, e_cols].bitcast(FP8X4),
                lhsT_scale=k_scales[:, e_cols],
                rhs=codes[:, g * P : (g + 1) * P].bitcast(FP8X4),
                rhs_scale=scales[:, g * P : (g + 1) * P],
                start=(g == 0),
                stop=(g == TOKEN_PASSES - 1),
            )

        def round_state(m):
            vk_grouped = vk_pool.tile([P, P, PACK], BF16, tag="vk_grouped", align_bytes=64)
            nc.scalar.copy(out=vk_grouped[:], in_=vk_sums[m][:].rearrange("p t d -> p d t"))
            vk_rounded[m] = vk_grouped

        def quantise_state(m):
            cols = slice(m * P, (m + 1) * P)
            nc.vector.quantize_mx(
                out=vk_codes[:, cols].bitcast(FP8X4),
                scales=vk_scales[:, cols],
                in_=vk_rounded[m][:].rearrange("p d t -> p (d t)"),
            )

        q_grouped = {}
        den_sums = {}
        repeated = {}

        def load_q(r):
            nc.sync.dma_start(
                out=q_ranges[r][:],
                in_=q_rows.rearrange("(t p) n -> p t n", p=P)[:, :, r * RANGE : (r + 1) * RANGE],
            )

        def relu_q(r):
            nc.vector.tensor_scalar_max(out=q_ranges[r][:], in0=q_ranges[r][:], scalar1=0.0)

        def regroup_q(r):
            grouped = grouped_pool.tile([P, PACK * RANGE], BF16, tag="grouped", align_bytes=64)
            half = RANGE // 2
            for side in range(2):
                dst = grouped[:, side * PACK * half : (side + 1) * PACK * half].rearrange(
                    "p (c i t) -> p c t i", i=RUN, t=PACK
                )
                src = q_ranges[r][:, :, side * half : (side + 1) * half].rearrange("p t (c i) -> p c t i", i=RUN)
                if side == 0:
                    nc.vector.tensor_copy(out=dst, in_=src)
                else:
                    nc.scalar.copy(out=dst, in_=src)
            q_grouped[r] = grouped

        def quantise_q(r):
            cols = slice(r * RANGE, (r + 1) * RANGE)
            nc.vector.quantize_mx(out=q_codes[:, cols].bitcast(FP8X4), scales=q_scales[:, cols], in_=q_grouped[r][:])

        def den_matmuls(r):
            den_ps = new_bank([P, RANGE_TILES, DEN_COLS])
            for j in range(RANGE_TILES):
                for t in range(E_TILES):
                    nc.tensor.matmul(
                        out=den_ps[:, j, :],
                        lhsT=q_ranges[r][:, t, j * P : (j + 1) * P],
                        rhs=pieces[:, t, :],
                        start=(t == 0),
                        stop=(t == E_TILES - 1),
                    )
            den_sums[r] = den_ps

        def reciprocal_den(r):
            nc.vector.tensor_reduce(out=den[:, r, :], in_=den_sums[r][:, :, 0:KSUM_PIECES], axis=AXIS.X, op=ALU.add)
            nc.vector.reciprocal(out=rden[:, r, :], in_=den[:, r, :])
            rep = rep_pool.tile([P, RANGE_TILES, P], F32)
            nc.gpsimd.tensor_scalar(
                out=rep[:],
                in0=rden[:, r, :].unsqueeze(2).to_broadcast([P, RANGE_TILES, P]),
                scalar1=1.0,
                scalar2=0.0,
                op0=ALU.mult,
                op1=ALU.add,
            )
            repeated[r] = rep

        def spread_den(r):
            for h in range(RANGE_BANKS):
                bank = new_bank([P, N_TILE // P, P])
                for square in range(N_TILE // P):
                    nc.tensor.transpose(
                        bank[:, square, :], repeated[r][:, h * (N_TILE // P) + square, :], ident_f32[:]
                    )
                first = r * RANGE + h * N_TILE
                nc.scalar.copy(out=rden_all[:, first : first + N_TILE], in_=bank[:].rearrange("p i c -> p (i c)"))

        k_tiles = {}
        k_grouped = {}

        def prepare_k(t):
            kr = k_tiles[t]
            for c in range(K_PARTS):
                nc.vector.tensor_scalar(
                    out=kr[:, c * K_PART : (c + 1) * K_PART],
                    in0=kr[:, c * K_PART : (c + 1) * K_PART],
                    scalar1=0.0,
                    scalar2=None,
                    op0=ALU.max,
                    op1=ALU.add,
                    accum_out=ksum_parts[:, t, c : c + 1],
                )
            k_grouped[t] = tokens_to_partitions(kr)

        def quantise_k(t):
            cols = slice(t * TOKEN_PASSES * P, (t + 1) * TOKEN_PASSES * P)
            nc.vector.quantize_mx(out=k_codes[:, cols].bitcast(FP8X4), scales=k_scales[:, cols], in_=k_grouped[t][:])

        def split_ksum():
            nc.vector.tensor_reduce(out=ksum[:], in_=ksum_parts[:], axis=AXIS.X, op=ALU.add)
            nc.vector.memset(pieces[:], 0.0)
            nc.vector.tensor_copy(out=pieces[:, :, 0], in_=ksum[:])
            nc.vector.tensor_sub(out=rest1[:], in0=ksum[:], in1=pieces[:, :, 0])
            nc.vector.tensor_copy(out=pieces[:, :, 1], in_=rest1[:])
            nc.vector.tensor_sub(out=rest2[:], in0=rest1[:], in1=pieces[:, :, 1])
            nc.vector.tensor_copy(out=pieces[:, :, 2], in_=rest2[:])

        results = {}

        def output_pass(m, r, h):
            if h == 0:
                results[(m, r)] = staging.tile([P, RANGE], F32, tag="result", name="result")
            d_cols = slice(m * P, (m + 1) * P)
            n_cols = slice(r * RANGE + h * N_TILE, r * RANGE + (h + 1) * N_TILE)
            num = new_bank([P, N_TILE])
            nc.tensor.matmul_mx(
                out=num[:],
                lhsT=vk_codes[:, d_cols].bitcast(FP8X4),
                lhsT_scale=vk_scales[:, d_cols],
                rhs=q_codes[:, n_cols].bitcast(FP8X4),
                rhs_scale=q_scales[:, n_cols],
                start=True,
                stop=True,
            )
            part = results[(m, r)][:, h * N_TILE : (h + 1) * N_TILE]
            if (RANGE_BANKS * (m + r) + h) % 3 == 1:
                nc.scalar.copy(out=part, in_=num[:])
                nc.gpsimd.tensor_mul(out=part, in0=part, in1=rden_all[:, n_cols])
            else:
                nc.vector.tensor_mul(out=part, in0=num[:], in1=rden_all[:, n_cols])
            if h == RANGE_BANKS - 1:
                nc.sync.dma_start(out=out_rows[d_cols, r * RANGE : (r + 1) * RANGE], in_=results[(m, r)][:])

        def is_k_tile(t):
            return 0 <= t < E_TILES

        def is_tile(m):
            return 0 <= m < D_TILES

        def is_range(r):
            return 0 <= r < Q_RANGES

        def work_round(p):
            if is_k_tile(p + E_TILES):
                prepare_k(p + E_TILES)
            if is_k_tile(p + E_TILES - 1) and p + E_TILES - 1 != E_TILES - 1:
                quantise_k(p + E_TILES - 1)
            if is_tile(p + 2):
                transpose_v(p + 2)
                if p + 2 + V_BUFS < D_TILES:
                    load_v(p + 2 + V_BUFS)
            if is_range(p - 1):
                spread_den(p - 1)
            if p == FIRST_STATE_ROUND:
                quantise_v(0)
                quantise_k(E_TILES - 1)
            if p == FIRST_STATE_ROUND + 1:
                split_ksum()
            if is_range(p):
                regroup_q(p)
            if is_range(p + 1):
                relu_q(p + 1)
            if is_tile(p):
                quantise_state(p)
            if is_range(p):
                den_matmuls(p)
                reciprocal_den(p)
            blocks = []
            if is_range(p - 1):
                blocks = blocks + [(m, p - 1) for m in range(p - 1)]
            if is_tile(p - 1):
                blocks = blocks + [(p - 1, r) for r in range(min(p, Q_RANGES))]
            passes = [(m, r, h) for m, r in blocks for h in range(RANGE_BANKS)]
            share = (len(passes) + STEPS - 1) // STEPS
            if is_tile(p + 1):
                for s in range(STEPS):
                    for i in range(s * STATE_PASSES // STEPS, (s + 1) * STATE_PASSES // STEPS):
                        state_pass(p + 1, i)
                    for m, r, h in passes[share * s : share * (s + 1)]:
                        output_pass(m, r, h)
                    if s == STEPS // 2 - 1 and is_tile(p + 2):
                        quantise_v(p + 2)
                round_state(p + 1)
            else:
                for m, r, h in passes:
                    output_pass(m, r, h)
            if is_range(p):
                quantise_q(p)

        with tc.tile_pool(name="k_in", bufs=E_TILES) as k_in:
            for t in range(E_TILES):
                k_tiles[t] = k_in.tile([P, N], BF16, name="k_sb")
                for c in range(K_PARTS):
                    nc.sync.dma_start(
                        out=k_tiles[t][:, c * K_PART : (c + 1) * K_PART],
                        in_=k_rows[t * P : (t + 1) * P, c * K_PART : (c + 1) * K_PART],
                    )
            load_v(0)
            load_v(1)
            load_q(0)
            for r in range(1, Q_RANGES):
                load_q(r)
                load_v(r + 1)
            for m in range(Q_RANGES + 1, V_BUFS):
                load_v(m)
            for p in range(FIRST_ROUND, 0):
                work_round(p)
        staging = ctx.enter_context(tc.tile_pool(name="staging", bufs=STAGING_BUFS))
        for p in range(0, LAST_ROUND + 1):
            work_round(p)
